import numpy as np
import ml_dtypes


def mxq(x, axis, fmt="e4m3"):
    dtype, down = {"e4m3": (ml_dtypes.float8_e4m3fn, 7), "e5m2": (ml_dtypes.float8_e5m2, 14)}[fmt]
    v = np.moveaxis(np.asarray(x, np.float32).astype(ml_dtypes.bfloat16).astype(np.float64), axis, -1)
    blocks = v.reshape(v.shape[:-1] + (-1, 32))
    amax = np.abs(blocks).max(-1, keepdims=True)
    byte = np.maximum(np.where(amax > 0, np.frexp(amax)[1] - 1 + 127, 0) - down, 1)
    scale = np.exp2(byte - 127.0)
    codes = (blocks / scale).astype(np.float32).astype(dtype).astype(np.float64)
    return np.moveaxis((codes * scale).reshape(v.shape), -1, axis)


WIDE = False


def mx_kscale(k):
    if not WIDE:
        return np.ones(k)
    levels = np.array([10, -10, 5, -5, 0])
    if k % 512:
        return np.exp2(np.random.permutation(np.resize(levels, k // 32))).repeat(32)
    a = np.empty((k // 512, 16))
    for p in range(k // 512):
        a[p, :8] = np.random.permutation(np.resize(levels, 8))
        for g in range(8):
            far = levels[np.abs(levels - a[p, g]) >= 10]
            a[p, g + 8] = far[np.random.randint(len(far))]
    return np.exp2(a.ravel()).repeat(32)


BF16 = ml_dtypes.bfloat16


def bf(x):
    return np.asarray(x, np.float32).astype(BF16)


def f64(x):
    return np.asarray(x).astype(np.float64)


E2M1 = np.array([0.0, 0.5, 1.0, 1.5, 2.0, 3.0, 4.0, 6.0, -0.0, -0.5, -1.0, -1.5, -2.0, -3.0, -4.0, -6.0])


def pack_weight(w, fmt):
    k, n = w.shape
    w = f64(bf(w)).reshape(k // 32, 32, n)
    amax = np.abs(w).max(1)
    if fmt == "e4m3":
        byte = np.frexp(amax)[1] - 1 + 127 - 7
    else:
        mant, ex = np.frexp(amax / 6.0)
        byte = np.where(mant > 0.5, ex, ex - 1) + 127
    byte = np.clip(np.where(amax > 0, byte, 1), 1, 254)
    scaled = (w * np.exp2(127.0 - byte)[:, None, :]).reshape(k, n).astype(np.float32)
    by_word = np.ascontiguousarray(scaled.reshape(k // 512, 128, 4, n).transpose(0, 1, 3, 2))
    if fmt == "e4m3":
        words = by_word.astype(ml_dtypes.float8_e4m3fn).view(np.uint8)
    else:
        c = by_word.astype(ml_dtypes.float4_e2m1fn).view(np.uint8) & 0xF
        words = c[..., 0::2] | (c[..., 1::2] << 4)
    return np.ascontiguousarray(words), np.ascontiguousarray(byte.astype(np.uint8).reshape(k // 512, 16, n))


def unpack_weight(words, scales, fmt):
    g, p, n, _ = words.shape
    if fmt == "e4m3":
        vals = np.ascontiguousarray(words).view(ml_dtypes.float8_e4m3fn).astype(np.float64)
    else:
        nib = np.empty((g, p, n, 4), np.uint8)
        nib[..., 0::2] = words & 0xF
        nib[..., 1::2] = words >> 4
        vals = E2M1[nib]
    vals = vals * np.repeat(np.exp2(scales.astype(np.float64) - 127.0), 8, axis=1)[..., None]
    return vals.transpose(0, 1, 3, 2).reshape(g * 512, n)
def pack4(w):
    words, scales = pack_weight(w, "e2m1")
    return words.reshape(words.shape[0], 128, -1), scales


def unpack4(words, scales):
    return unpack_weight(words.reshape(words.shape[0], 128, -1, 2), scales, "e2m1")


B, T, E = 32, 256, 512


def draw0():
    s, t = mx_kscale(E), mx_kscale(E)
    r = np.random.standard_normal
    x1, x2 = bf(r((B, T, E)) * s), bf(r((B, T, E)) * s)
    W1_words, W1_scales = pack4(r((E, E)) * 0.4 / np.sqrt(E) / s[:, None] * t)
    W2_words, W2_scales = pack4(r((E, E)) * 0.4 / np.sqrt(E) / s[:, None] / t)
    return {"x1": x1, "x2": x2,
            "W1_words": W1_words, "W1_scales": W1_scales, "W2_words": W2_words, "W2_scales": W2_scales,
            "b1": bf(r((T, E)) * 0.1 * t), "b2": bf(r((T, E)) * 0.1 / t)}


def core(x1, x2, W1_words, W1_scales, W2_words, W2_scales, b1, b2):
    e1t = np.maximum((mxq(f64(x1), 2, "e4m3") @ unpack4(W1_words, W1_scales)) + f64(b1), 0.0)
    e2t = np.maximum((mxq(f64(x2), 2, "e4m3") @ unpack4(W2_words, W2_scales)) + f64(b2), 0.0)
    scores = mxq(e2t, 2, "e4m3") @ mxq(e1t, 2, "e4m3").transpose(0, 2, 1)
    ex = np.exp(scores - scores.max(-1, keepdims=True))
    return ex / ex.sum(-1, keepdims=True)


def e4m3fn_bytes(y):
    return np.clip(np.asarray(y, np.float64), -448.0, 448.0).astype(np.float32).astype(ml_dtypes.float8_e4m3fn).view(np.uint8)


def e4m3fn_values(b):
    return np.asarray(b, np.uint8).view(ml_dtypes.float8_e4m3fn).astype(np.float64)


def setup_inputs():
    d = draw0()
    x0 = np.asarray(d['x2']).astype(np.float64)
    s = (np.max(np.abs(x0), axis=(0, 1), keepdims=True) / 448.0).astype(np.float32)
    out = {}
    for k, v in d.items():
        if k == 'x2':
            out['x2_bytes'] = e4m3fn_bytes(x0 / s.astype(np.float64))
            out['x2_scale'] = s
        else:
            out[k] = v
    return out


def reference(x1, x2_bytes, x2_scale, W1_words, W1_scales, W2_words, W2_scales, b1, b2):
    return core(x1, e4m3fn_values(x2_bytes) * x2_scale.astype(np.float64), W1_words, W1_scales, W2_words, W2_scales, b1, b2)

@@ -1,0 +1,259 @@
+from contextlib import ExitStack
+
+import concourse.mybir as mybir
+from concourse.masks import make_identity
+
+B, T, E = 32, 256, 512
+P = 128
+FLOPS = 2 * B * (2 * T * E * E + T * T * E)
+
+F32 = mybir.dt.float32
+BF16 = mybir.dt.bfloat16
+I32 = mybir.dt.int32
+U32 = mybir.dt.uint32
+U8 = mybir.dt.uint8
+FP8 = mybir.dt.float8_e4m3fn
+FP8X4 = mybir.dt.float8_e4m3fn_x4
+FP4X4 = mybir.dt.float4_e2m1fn_x4
+ACT = mybir.ActivationFunctionType
+ALU = mybir.AluOpType
+AX = mybir.AxisListType
+
+AHEAD_LOAD = 6
+
+
+def tile_attentionmm_pa_t_w4_kernel(tc, x1, x2_bytes, x2_scale, W1_words, W1_scales, W2_words, W2_scales, b1, b2, out):
+    nc = tc.nc
+    with ExitStack() as ctx:
+        const = ctx.enter_context(tc.tile_pool(name="const", bufs=1))
+        loads = ctx.enter_context(tc.tile_pool(name="loads", bufs=AHEAD_LOAD + 1))
+        work = ctx.enter_context(tc.tile_pool(name="work", bufs=3))
+        ps_x = ctx.enter_context(tc.psum_pool(name="ps_x", bufs=1))
+        ps_e = ctx.enter_context(tc.psum_pool(name="ps_e", bufs=1))
+        ps_s = ctx.enter_context(tc.psum_pool(name="ps_s", bufs=2))
+
+        ident = const.tile([P, P], F32, name="ident")
+        scale_row = const.tile([P, 2, E], F32, name="scale_row")
+        bias_raw = const.tile([P, 2, 2, E], BF16, name="bias_raw")
+        bias = const.tile([P, 2, T, 4], BF16, name="bias", align_bytes=64)
+        w_in = const.tile([P, 2, 2 * E], U8, name="w_in", align_bytes=64)
+        w_codes = const.tile([P, 2, 2 * E], U8, name="w_codes", align_bytes=64)
+        ws_in = const.tile([P, 2, E], U8, name="ws_in", align_bytes=64)
+        w_scales = const.tile([P, 2, E], U8, name="w_scales", align_bytes=64)
+
+        live = {}
+
+        def load(b):
+            x1_rows = loads.tile([P, 2, E], BF16, name="x1_rows", tag="x1_rows")
+            x2_codes = loads.tile([P, 2, E], U8, name="x2_codes", tag="x2_codes")
+            nc.sync.dma_start(out=x2_codes[:], in_=x2_bytes[b].rearrange("(r i) k -> r i k", i=2))
+            nc.sync.dma_start(out=x1_rows[:], in_=x1[b].rearrange("(i r) k -> r i k", i=2))
+            live["x1", b] = x1_rows
+            live["x2c", b] = x2_codes
+
+        def widen(b):
+            codes = live.pop(("x2c", b))
+            x2_wide = work.tile([P, 2, E], BF16, name="x2_wide", tag="x2_wide")
+            nc.scalar.copy(
+                out=x2_wide[:].rearrange("p i k -> p (i k)"),
+                in_=codes[:].rearrange("p i k -> p (i k)").bitcast(FP8),
+            )
+            live["x2w", b] = x2_wide
+
+        def scale_x2(b):
+            x2_wide = live.pop(("x2w", b))
+            x2_rows = work.tile([P, 2, E], BF16, name="x2_rows", tag="x2_rows")
+            for i in range(2):
+                for c in range(0, E, 256):
+                    nc.gpsimd.tensor_tensor(
+                        out=x2_rows[:, i, c : c + 256], in0=x2_wide[:, i, c : c + 256], in1=scale_row[:, i, c : c + 256], op=ALU.mult
+                    )
+            live["x2", b] = x2_rows
+
+        def transpose_rows(rows, s):
+            words_t = ps_x.tile([P, 2, T], F32, name="words_t", tag="words_t%d" % s)
+            for u in range(2):
+                for i in range(2):
+                    words = rows[:, i, :].bitcast(F32)
+                    nc.tensor.transpose(words_t[:, u, i * P : (i + 1) * P], words[:, u : E // 2 : 2], ident[:])
+            return words_t
+
+        def empty_words(words_t, dst):
+            nc.scalar.copy(
+                out=dst.rearrange("p n j -> p (n j)").bitcast(F32).rearrange("p (n u) -> p n u", u=2),
+                in_=words_t[:].rearrange("p u n -> p n u"),
+            )
+
+        def transpose_x(b):
+            live["t1", b] = transpose_rows(live.pop(("x1", b)), 0)
+            live["t2", b] = transpose_rows(live.pop(("x2", b)), 1)
+
+        def empty_x(b):
+            x_bf = work.tile([P, 2, T, 4], BF16, name="x_bf", tag="x_bf", align_bytes=64)
+            empty_words(live.pop(("t1", b)), x_bf[:, 0])
+            empty_words(live.pop(("t2", b)), x_bf[:, 1])
+            live["xb", b] = x_bf
+
+        def quantize(src):
+            codes = work.tile([P, 2 * T], U32, name="codes", tag="codes", bufs=6, align_bytes=64)
+            scales = work.tile([P, 2 * T], U8, name="scales", tag="scales", bufs=6, align_bytes=64)
+            nc.vector.quantize_mx(
+                out=codes[:].bitcast(FP8X4), scales=scales[:], in_=src[:].rearrange("p s n j -> p (s n j)")
+            )
+            return codes, scales
+
+        def matmul_e(b, s, h):
+            codes, scales = live["xq", b]
+            acc = ps_e.tile([P, 4, P], F32, name="acc", tag="acc%d%d" % (s, h))
+            cols = slice(s * T + h * P, s * T + (h + 1) * P)
+            for j in range(4):
+                nc.tensor.matmul_mx(
+                    out=acc[:, j, :],
+                    lhsT=w_codes[:, s, 2 * P * j : 2 * P * (j + 1)].bitcast(FP4X4),
+                    lhsT_scale=w_scales[:, s, P * j : P * (j + 1)],
+                    rhs=codes[:, cols].bitcast(FP8X4),
+                    rhs_scale=scales[:, cols],
+                    start=True,
+                    stop=True,
+                )
+            live["acc", b, s, h] = acc
+
+        def add_bias(b, s, h):
+            if ("z", b) not in live:
+                z_bf = work.tile([P, 2, T, 4], BF16, name="z_bf", tag="z_bf", align_bytes=64)
+                live["z", b] = z_bf
+            rows = slice(h * P, (h + 1) * P)
+            nc.vector.tensor_tensor(
+                out=live["z", b][:, s, rows, :],
+                in0=live.pop(("acc", b, s, h))[:].rearrange("p j n -> p n j"),
+                in1=bias[:, s, rows, :],
+                op=ALU.add,
+            )
+
+        def relu(b, s, h0, h1, on_vector):
+            if ("e", b) not in live:
+                e_bf = work.tile([P, 2, T, 4], BF16, name="e_bf", tag="e_bf", align_bytes=64)
+                live["e", b] = e_bf
+            src = live["z", b][:, s, h0 * P : h1 * P, :].rearrange("p n j -> p (n j)")
+            dst = live["e", b][:, s, h0 * P : h1 * P, :].rearrange("p n j -> p (n j)")
+            if on_vector:
+                nc.vector.tensor_scalar(out=dst, in0=src, scalar1=0.0, scalar2=None, op0=ALU.max)
+            else:
+                nc.scalar.activation(out=dst, in_=src, func=ACT.Relu)
+
+        def scores(b):
+            codes, scales = live.pop(("eq", b))
+            sc = ps_s.tile([P, 2, T], F32, name="sc", tag="sc")
+            for i in range(2):
+                cols = slice(T + i * P, T + (i + 1) * P)
+                nc.tensor.matmul_mx(
+                    out=sc[:, i, :],
+                    lhsT=codes[:, cols].bitcast(FP8X4),
+                    lhsT_scale=scales[:, cols],
+                    rhs=codes[:, 0:T].bitcast(FP8X4),
+                    rhs_scale=scales[:, 0:T],
+                    start=True,
+                    stop=True,
+                )
+            live["sc", b] = sc
+
+        def row_max(b):
+            neg_max = work.tile([P, 2], F32, name="neg_max", tag="neg_max")
+            nc.vector.tensor_reduce(out=neg_max[:], in_=live["sc", b][:], axis=AX.X, op=ALU.max, negate=True)
+            live["nm", b] = neg_max
+
+        def exps(b):
+            sc = live.pop(("sc", b))
+            neg_max = live.pop(("nm", b))
+            ex = work.tile([P, 2, T], F32, name="ex", tag="ex")
+            sums = work.tile([P, 2], F32, name="sums", tag="sums")
+            for i in range(2):
+                nc.scalar.activation(
+                    out=ex[:, i, :], in_=sc[:, i, :], func=ACT.Exp, bias=neg_max[:, i : i + 1], accum_out=sums[:, i : i + 1]
+                )
+            live["ex", b] = ex
+            live["sums", b] = sums
+
+        def recip(b):
+            inv = work.tile([P, 2], F32, name="inv", tag="inv")
+            nc.vector.reciprocal(out=inv[:], in_=live.pop(("sums", b))[:])
+            live["inv", b] = inv
+
+        def normalise(b):
+            ex = live.pop(("ex", b))
+            inv = live.pop(("inv", b))
+            probs = work.tile([P, 2, T], F32, name="probs", tag="probs")
+            for i in range(2):
+                nc.gpsimd.tensor_scalar(
+                    out=probs[:, i, :], in0=ex[:, i, :], scalar1=inv[:, i : i + 1], scalar2=1.0, op0=ALU.mult, op1=ALU.mult
+                )
+            nc.sync.dma_start(out=out[b].rearrange("(r i) j -> r i j", i=2), in_=probs[:])
+
+        with tc.manual_schedule():
+            nc.vector.memset(ws_in[:].rearrange("p s n -> p (s n)").bitcast(I32), 0)
+            make_identity(nc, ident[:])
+            load(0)
+            nc.sync.dma_start(out=scale_row[:, 0, :], in_=x2_scale.rearrange("a c k -> (a c k)").partition_broadcast(P))
+            nc.sync.dma_start(out=bias_raw[:, 0], in_=b1.rearrange("(i r) k -> r i k", i=2))
+            nc.sync.dma_start(out=bias_raw[:, 1], in_=b2.rearrange("(r i) k -> r i k", i=2))
+            nc.sync.dma_start(out=w_in[:, 0, :], in_=W1_words[0])
+            nc.sync.dma_start(out=w_in[:, 1, :], in_=W2_words[0])
+            for s, w_s in enumerate((W1_scales, W2_scales)):
+                for q in range(4):
+                    nc.sync.dma_start(
+                        out=ws_in[32 * q : 32 * q + 4, s, :].bitcast(I32), in_=w_s[0, 4 * q : 4 * q + 4, :].bitcast(I32)
+                    )
+            for b in range(1, AHEAD_LOAD):
+                load(b)
+            nc.scalar.copy(out=scale_row[:, 1, :], in_=scale_row[:, 0, :])
+            for s in range(2):
+                empty_words(transpose_rows(bias_raw[:, s], s), bias[:, s])
+            for s in range(2):
+                nc.vector.tensor_copy(
+                    out=w_codes[:, s, :].rearrange("p (j m c) -> p j m c", j=4, c=2),
+                    in_=w_in[:, s, :].rearrange("p (m j c) -> p j m c", j=4, c=2),
+                )
+                nc.vector.tensor_copy(
+                    out=w_scales[:, s, :].rearrange("p (j m) -> p j m", j=4),
+                    in_=ws_in[:, s, :].rearrange("p (m j) -> p j m", j=4),
+                )
+
+            def ok(b):
+                return 0 <= b < B
+
+            for i in range(-4, B + 3):
+                if ok(i + AHEAD_LOAD) and i >= 0:
+                    load(i + AHEAD_LOAD)
+                if ok(i + 3):
+                    scale_x2(i + 3)
+                if ok(i + 2):
+                    empty_x(i + 2)
+                for s in range(2):
+                    if ok(i):
+                        add_bias(i, s, 0)
+                    if s == 0 and ok(i - 2):
+                        recip(i - 2)
+                        normalise(i - 2)
+                    if ok(i):
+                        add_bias(i, s, 1)
+                        if s == 0:
+                            relu(i, s, 0, 2, False)
+                        else:
+                            relu(i, s, 0, 1, False)
+                if ok(i - 1):
+                    row_max(i - 1)
+                    exps(i - 1)
+                if ok(i):
+                    relu(i, 1, 1, 2, True)
+                if ok(i + 4):
+                    widen(i + 4)
+                if ok(i + 1):
+                    live["xq", i + 1] = quantize(live.pop(("xb", i + 1)))
+                    for s in range(2):
+                        for h in range(2):
+                            matmul_e(i + 1, s, h)
+                if ok(i):
+                    live["eq", i] = quantize(live.pop(("e", i)))
+                    scores(i)
+                if ok(i + 3):
+                    transpose_x(i + 3)

@@ -53,21 +53,13 @@ def tile_attentionmm_pa_t_w4_kernel(tc, x1, x2_bytes, x2_scale, W1_words, W1_sca
 
         def widen(b):
             codes = live.pop(("x2c", b))
-            x2_wide = work.tile([P, 2, E], BF16, name="x2_wide", tag="x2_wide")
-            nc.scalar.copy(
-                out=x2_wide[:].rearrange("p i k -> p (i k)"),
-                in_=codes[:].rearrange("p i k -> p (i k)").bitcast(FP8),
-            )
-            live["x2w", b] = x2_wide
-
-        def scale_x2(b):
-            x2_wide = live.pop(("x2w", b))
             x2_rows = work.tile([P, 2, E], BF16, name="x2_rows", tag="x2_rows")
-            for i in range(2):
-                for c in range(0, E, 256):
-                    nc.gpsimd.tensor_tensor(
-                        out=x2_rows[:, i, c : c + 256], in0=x2_wide[:, i, c : c + 256], in1=scale_row[:, i, c : c + 256], op=ALU.mult
-                    )
+            nc.vector.tensor_tensor(
+                out=x2_rows[:].rearrange("p i k -> p (i k)"),
+                in0=codes[:].rearrange("p i k -> p (i k)").bitcast(FP8),
+                in1=scale_row[:].rearrange("p i k -> p (i k)"),
+                op=ALU.mult,
+            )
             live["x2", b] = x2_rows
 
         def transpose_rows(rows, s):
@@ -184,9 +176,7 @@ def tile_attentionmm_pa_t_w4_kernel(tc, x1, x2_bytes, x2_scale, W1_words, W1_sca
             inv = live.pop(("inv", b))
             probs = work.tile([P, 2, T], F32, name="probs", tag="probs")
             for i in range(2):
-                nc.gpsimd.tensor_scalar(
-                    out=probs[:, i, :], in0=ex[:, i, :], scalar1=inv[:, i : i + 1], scalar2=1.0, op0=ALU.mult, op1=ALU.mult
-                )
+                nc.scalar.activation(out=probs[:, i, :], in_=ex[:, i, :], func=ACT.Copy, scale=inv[:, i : i + 1])
             nc.sync.dma_start(out=out[b].rearrange("(r i) j -> r i j", i=2), in_=probs[:])
 
         with tc.manual_schedule():
@@ -224,10 +214,10 @@ def tile_attentionmm_pa_t_w4_kernel(tc, x1, x2_bytes, x2_scale, W1_words, W1_sca
             for i in range(-4, B + 3):
                 if ok(i + AHEAD_LOAD) and i >= 0:
                     load(i + AHEAD_LOAD)
-                if ok(i + 3):
-                    scale_x2(i + 3)
                 if ok(i + 2):
                     empty_x(i + 2)
+                if ok(i + 3):
+                    transpose_x(i + 3)
                 for s in range(2):
                     if ok(i):
                         add_bias(i, s, 0)
@@ -236,24 +226,17 @@ def tile_attentionmm_pa_t_w4_kernel(tc, x1, x2_bytes, x2_scale, W1_words, W1_sca
                         normalise(i - 2)
                     if ok(i):
                         add_bias(i, s, 1)
-                        if s == 0:
-                            relu(i, s, 0, 2, False)
-                        else:
-                            relu(i, s, 0, 1, False)
+                        relu(i, s, 0, 2, False)
                 if ok(i - 1):
                     row_max(i - 1)
                     exps(i - 1)
-                if ok(i):
-                    relu(i, 1, 1, 2, True)
-                if ok(i + 4):
-                    widen(i + 4)
                 if ok(i + 1):
                     live["xq", i + 1] = quantize(live.pop(("xb", i + 1)))
                     for s in range(2):
                         for h in range(2):
                             matmul_e(i + 1, s, h)
+                if ok(i + 4):
+                    widen(i + 4)
                 if ok(i):
                     live["eq", i] = quantize(live.pop(("e", i)))
                     scores(i)
-                if ok(i + 3):
-                    transpose_x(i + 3)

@@ -19,7 +19,7 @@ ACT = mybir.ActivationFunctionType
 ALU = mybir.AluOpType
 AX = mybir.AxisListType
 
-AHEAD_LOAD = 6
+AHEAD_LOAD = 8
 
 
 def tile_attentionmm_pa_t_w4_kernel(tc, x1, x2_bytes, x2_scale, W1_words, W1_scales, W2_words, W2_scales, b1, b2, out):
@@ -30,10 +30,11 @@ def tile_attentionmm_pa_t_w4_kernel(tc, x1, x2_bytes, x2_scale, W1_words, W1_sca
         work = ctx.enter_context(tc.tile_pool(name="work", bufs=3))
         ps_x = ctx.enter_context(tc.psum_pool(name="ps_x", bufs=1))
         ps_e = ctx.enter_context(tc.psum_pool(name="ps_e", bufs=1))
-        ps_s = ctx.enter_context(tc.psum_pool(name="ps_s", bufs=2))
+        ps_s = ctx.enter_context(tc.psum_pool(name="ps_s", bufs=1))
 
         ident = const.tile([P, P], F32, name="ident")
-        scale_row = const.tile([P, 2, E], F32, name="scale_row")
+        ident_bf = const.tile([P, P], BF16, name="ident_bf")
+        scale_cols = const.tile([P, 4], F32, name="scale_cols")
         bias_raw = const.tile([P, 2, 2, E], BF16, name="bias_raw")
         bias = const.tile([P, 2, T, 4], BF16, name="bias", align_bytes=64)
         w_in = const.tile([P, 2, 2 * E], U8, name="w_in", align_bytes=64)
@@ -54,11 +55,9 @@ def tile_attentionmm_pa_t_w4_kernel(tc, x1, x2_bytes, x2_scale, W1_words, W1_sca
         def widen(b):
             codes = live.pop(("x2c", b))
             x2_rows = work.tile([P, 2, E], BF16, name="x2_rows", tag="x2_rows")
-            nc.vector.tensor_tensor(
+            nc.scalar.copy(
                 out=x2_rows[:].rearrange("p i k -> p (i k)"),
-                in0=codes[:].rearrange("p i k -> p (i k)").bitcast(FP8),
-                in1=scale_row[:].rearrange("p i k -> p (i k)"),
-                op=ALU.mult,
+                in_=codes[:].rearrange("p i k -> p (i k)").bitcast(FP8),
             )
             live["x2", b] = x2_rows
 
@@ -80,19 +79,56 @@ def tile_attentionmm_pa_t_w4_kernel(tc, x1, x2_bytes, x2_scale, W1_words, W1_sca
             live["t1", b] = transpose_rows(live.pop(("x1", b)), 0)
             live["t2", b] = transpose_rows(live.pop(("x2", b)), 1)
 
-        def empty_x(b):
-            x_bf = work.tile([P, 2, T, 4], BF16, name="x_bf", tag="x_bf", align_bytes=64)
+        def exit_x1(b):
+            x_bf = work.tile([P, 2, T, 4], BF16, name="x_bf", tag="x_bf", bufs=4, align_bytes=64)
             empty_words(live.pop(("t1", b)), x_bf[:, 0])
-            empty_words(live.pop(("t2", b)), x_bf[:, 1])
             live["xb", b] = x_bf
 
-        def quantize(src):
+        def exit_scale(b):
+            words = live.pop(("t2", b))[:].rearrange("p u n -> p (u n)").bitcast(BF16)
+            pairs = words.rearrange("p (u n e) -> p u e n", u=2, e=2)
+            planes = work.tile([P, 4, T], BF16, name="planes", tag="planes")
+            for t in range(4):
+                nc.scalar.activation(
+                    out=planes[:, t, :], in_=pairs[:, t // 2, t % 2, :], func=ACT.Copy, scale=scale_cols[:, t : t + 1]
+                )
+            live["pl", b] = planes
+
+        def interleave(b):
+            planes = live.pop(("pl", b))
+            if b == 0:
+                nc.vector.tensor_copy(out=live["xb", b][:, 1], in_=planes[:].rearrange("p t n -> p n t"))
+                return
+            hop = ps_x.tile([P, T, 4], BF16, name="hop", tag="hop")
+            for h in range(2):
+                rows = slice(h * P, (h + 1) * P)
+                nc.tensor.matmul(
+                    hop[:, rows, :].rearrange("p n t -> p (n t)"),
+                    lhsT=ident_bf[:],
+                    rhs=planes[:, :, rows].rearrange("p t n -> p n t"),
+                    start=True,
+                    stop=True,
+                )
+            live["hop", b] = hop
+
+        def exit_hop(b):
+            if b > 0:
+                nc.scalar.copy(
+                    out=live["xb", b][:, 1].rearrange("p n t -> p (n t)"), in_=live.pop(("hop", b))[:].rearrange("p n t -> p (n t)")
+                )
+
+        def new_codes():
             codes = work.tile([P, 2 * T], U32, name="codes", tag="codes", bufs=6, align_bytes=64)
             scales = work.tile([P, 2 * T], U8, name="scales", tag="scales", bufs=6, align_bytes=64)
-            nc.vector.quantize_mx(
-                out=codes[:].bitcast(FP8X4), scales=scales[:], in_=src[:].rearrange("p s n j -> p (s n j)")
-            )
             return codes, scales
+
+        def quantize_part(src, dst, s0, s1):
+            codes, scales = dst
+            nc.vector.quantize_mx(
+                out=codes[:, s0 * T : s1 * T].bitcast(FP8X4),
+                scales=scales[:, s0 * T : s1 * T],
+                in_=src[:, s0:s1].rearrange("p s n j -> p (s n j)"),
+            )
 
         def matmul_e(b, s, h):
             codes, scales = live["xq", b]
@@ -182,8 +218,9 @@ def tile_attentionmm_pa_t_w4_kernel(tc, x1, x2_bytes, x2_scale, W1_words, W1_sca
         with tc.manual_schedule():
             nc.vector.memset(ws_in[:].rearrange("p s n -> p (s n)").bitcast(I32), 0)
             make_identity(nc, ident[:])
+            nc.gpsimd.tensor_copy(out=ident_bf[:], in_=ident[:])
             load(0)
-            nc.sync.dma_start(out=scale_row[:, 0, :], in_=x2_scale.rearrange("a c k -> (a c k)").partition_broadcast(P))
+            nc.sync.dma_start(out=scale_cols[:], in_=x2_scale.rearrange("a c (p t) -> p (a c t)", t=4))
             nc.sync.dma_start(out=bias_raw[:, 0], in_=b1.rearrange("(i r) k -> r i k", i=2))
             nc.sync.dma_start(out=bias_raw[:, 1], in_=b2.rearrange("(r i) k -> r i k", i=2))
             nc.sync.dma_start(out=w_in[:, 0, :], in_=W1_words[0])
@@ -195,7 +232,6 @@ def tile_attentionmm_pa_t_w4_kernel(tc, x1, x2_bytes, x2_scale, W1_words, W1_sca
                     )
             for b in range(1, AHEAD_LOAD):
                 load(b)
-            nc.scalar.copy(out=scale_row[:, 1, :], in_=scale_row[:, 0, :])
             for s in range(2):
                 empty_words(transpose_rows(bias_raw[:, s], s), bias[:, s])
             for s in range(2):
@@ -211,32 +247,42 @@ def tile_attentionmm_pa_t_w4_kernel(tc, x1, x2_bytes, x2_scale, W1_words, W1_sca
             def ok(b):
                 return 0 <= b < B
 
-            for i in range(-4, B + 3):
+            for i in range(-5, B + 3):
                 if ok(i + AHEAD_LOAD) and i >= 0:
                     load(i + AHEAD_LOAD)
                 if ok(i + 2):
-                    empty_x(i + 2)
+                    exit_x1(i + 2)
+                    exit_scale(i + 2)
+                    interleave(i + 2)
                 if ok(i + 3):
                     transpose_x(i + 3)
-                for s in range(2):
-                    if ok(i):
-                        add_bias(i, s, 0)
-                    if s == 0 and ok(i - 2):
-                        recip(i - 2)
-                        normalise(i - 2)
-                    if ok(i):
-                        add_bias(i, s, 1)
-                        relu(i, s, 0, 2, False)
-                if ok(i - 1):
-                    row_max(i - 1)
-                    exps(i - 1)
-                if ok(i + 1):
-                    live["xq", i + 1] = quantize(live.pop(("xb", i + 1)))
-                    for s in range(2):
-                        for h in range(2):
-                            matmul_e(i + 1, s, h)
+                if ok(i - 2):
+                    normalise(i - 2)
                 if ok(i + 4):
                     widen(i + 4)
                 if ok(i):
-                    live["eq", i] = quantize(live.pop(("e", i)))
+                    for s in range(2):
+                        for h in range(2):
+                            add_bias(i, s, h)
+                if ok(i - 1):
+                    row_max(i - 1)
+                    exps(i - 1)
+                if ok(i + 2):
+                    exit_hop(i + 2)
+                if ok(i):
+                    relu(i, 0, 0, 2, True)
+                if ok(i + 1):
+                    live["xq", i + 1] = new_codes()
+                    quantize_part(live.pop(("xb", i + 1)), live["xq", i + 1], 0, 2)
+                    for s in range(2):
+                        for h in range(2):
+                            matmul_e(i + 1, s, h)
+                if ok(i):
+                    relu(i, 1, 0, 2, True)
+                    live["eq", i] = new_codes()
+                    quantize_part(live["e", i], live["eq", i], 0, 1)
+                if ok(i - 1):
+                    recip(i - 1)
+                if ok(i):
+                    quantize_part(live.pop(("e", i)), live["eq", i], 1, 2)
                     scores(i)

from contextlib import ExitStack

import concourse.mybir as mybir
from concourse.masks import make_identity

B, T, E = 32, 256, 512
P = 128
FLOPS = 2 * B * (2 * T * E * E + T * T * E)

F32 = mybir.dt.float32
BF16 = mybir.dt.bfloat16
I32 = mybir.dt.int32
U32 = mybir.dt.uint32
U8 = mybir.dt.uint8
FP8 = mybir.dt.float8_e4m3fn
FP8X4 = mybir.dt.float8_e4m3fn_x4
FP4X4 = mybir.dt.float4_e2m1fn_x4
ACT = mybir.ActivationFunctionType
ALU = mybir.AluOpType
AX = mybir.AxisListType

AHEAD_LOAD = 8


def tile_attentionmm_pa_t_w4_kernel(tc, x1, x2_bytes, x2_scale, W1_words, W1_scales, W2_words, W2_scales, b1, b2, out):
    nc = tc.nc
    with ExitStack() as ctx:
        const = ctx.enter_context(tc.tile_pool(name="const", bufs=1))
        loads = ctx.enter_context(tc.tile_pool(name="loads", bufs=AHEAD_LOAD + 1))
        work = ctx.enter_context(tc.tile_pool(name="work", bufs=3))
        ps_x = ctx.enter_context(tc.psum_pool(name="ps_x", bufs=1))
        ps_e = ctx.enter_context(tc.psum_pool(name="ps_e", bufs=1))
        ps_s = ctx.enter_context(tc.psum_pool(name="ps_s", bufs=1))

        ident = const.tile([P, P], F32, name="ident")
        ident_bf = const.tile([P, P], BF16, name="ident_bf")
        scale_cols = const.tile([P, 4], F32, name="scale_cols")
        bias_raw = const.tile([P, 2, 2, E], BF16, name="bias_raw")
        bias = const.tile([P, 2, T, 4], BF16, name="bias", align_bytes=64)
        w_in = const.tile([P, 2, 2 * E], U8, name="w_in", align_bytes=64)
        w_codes = const.tile([P, 2, 2 * E], U8, name="w_codes", align_bytes=64)
        ws_in = const.tile([P, 2, E], U8, name="ws_in", align_bytes=64)
        w_scales = const.tile([P, 2, E], U8, name="w_scales", align_bytes=64)

        live = {}

        def load(b):
            x1_rows = loads.tile([P, 2, E], BF16, name="x1_rows", tag="x1_rows")
            x2_codes = loads.tile([P, 2, E], U8, name="x2_codes", tag="x2_codes")
            nc.sync.dma_start(out=x2_codes[:], in_=x2_bytes[b].rearrange("(r i) k -> r i k", i=2))
            nc.sync.dma_start(out=x1_rows[:], in_=x1[b].rearrange("(i r) k -> r i k", i=2))
            live["x1", b] = x1_rows
            live["x2c", b] = x2_codes

        def widen(b):
            codes = live.pop(("x2c", b))
            x2_rows = work.tile([P, 2, E], BF16, name="x2_rows", tag="x2_rows")
            nc.scalar.copy(
                out=x2_rows[:].rearrange("p i k -> p (i k)"),
                in_=codes[:].rearrange("p i k -> p (i k)").bitcast(FP8),
            )
            live["x2", b] = x2_rows

        def transpose_rows(rows, s):
            words_t = ps_x.tile([P, 2, T], F32, name="words_t", tag="words_t%d" % s)
            for u in range(2):
                for i in range(2):
                    words = rows[:, i, :].bitcast(F32)
                    nc.tensor.transpose(words_t[:, u, i * P : (i + 1) * P], words[:, u : E // 2 : 2], ident[:])
            return words_t

        def empty_words(words_t, dst):
            nc.scalar.copy(
                out=dst.rearrange("p n j -> p (n j)").bitcast(F32).rearrange("p (n u) -> p n u", u=2),
                in_=words_t[:].rearrange("p u n -> p n u"),
            )

        def transpose_x(b):
            live["t1", b] = transpose_rows(live.pop(("x1", b)), 0)
            live["t2", b] = transpose_rows(live.pop(("x2", b)), 1)

        def exit_x1(b):
            x_bf = work.tile([P, 2, T, 4], BF16, name="x_bf", tag="x_bf", bufs=4, align_bytes=64)
            empty_words(live.pop(("t1", b)), x_bf[:, 0])
            live["xb", b] = x_bf

        def exit_scale(b):
            words = live.pop(("t2", b))[:].rearrange("p u n -> p (u n)").bitcast(BF16)
            pairs = words.rearrange("p (u n e) -> p u e n", u=2, e=2)
            planes = work.tile([P, 4, T], BF16, name="planes", tag="planes")
            for t in range(4):
                nc.scalar.activation(
                    out=planes[:, t, :], in_=pairs[:, t // 2, t % 2, :], func=ACT.Copy, scale=scale_cols[:, t : t + 1]
                )
            live["pl", b] = planes

        def interleave(b):
            planes = live.pop(("pl", b))
            if b == 0:
                nc.vector.tensor_copy(out=live["xb", b][:, 1], in_=planes[:].rearrange("p t n -> p n t"))
                return
            hop = ps_x.tile([P, T, 4], BF16, name="hop", tag="hop")
            for h in range(2):
                rows = slice(h * P, (h + 1) * P)
                nc.tensor.matmul(
                    hop[:, rows, :].rearrange("p n t -> p (n t)"),
                    lhsT=ident_bf[:],
                    rhs=planes[:, :, rows].rearrange("p t n -> p n t"),
                    start=True,
                    stop=True,
                )
            live["hop", b] = hop

        def exit_hop(b):
            if b > 0:
                nc.scalar.copy(
                    out=live["xb", b][:, 1].rearrange("p n t -> p (n t)"), in_=live.pop(("hop", b))[:].rearrange("p n t -> p (n t)")
                )

        def new_codes():
            codes = work.tile([P, 2 * T], U32, name="codes", tag="codes", bufs=6, align_bytes=64)
            scales = work.tile([P, 2 * T], U8, name="scales", tag="scales", bufs=6, align_bytes=64)
            return codes, scales

        def quantize_part(src, dst, s0, s1):
            codes, scales = dst
            nc.vector.quantize_mx(
                out=codes[:, s0 * T : s1 * T].bitcast(FP8X4),
                scales=scales[:, s0 * T : s1 * T],
                in_=src[:, s0:s1].rearrange("p s n j -> p (s n j)"),
            )

        def matmul_e(b, s, h):
            codes, scales = live["xq", b]
            acc = ps_e.tile([P, 4, P], F32, name="acc", tag="acc%d%d" % (s, h))
            cols = slice(s * T + h * P, s * T + (h + 1) * P)
            for j in range(4):
                nc.tensor.matmul_mx(
                    out=acc[:, j, :],
                    lhsT=w_codes[:, s, 2 * P * j : 2 * P * (j + 1)].bitcast(FP4X4),
                    lhsT_scale=w_scales[:, s, P * j : P * (j + 1)],
                    rhs=codes[:, cols].bitcast(FP8X4),
                    rhs_scale=scales[:, cols],
                    start=True,
                    stop=True,
                )
            live["acc", b, s, h] = acc

        def add_bias(b, s, h):
            if ("z", b) not in live:
                z_bf = work.tile([P, 2, T, 4], BF16, name="z_bf", tag="z_bf", align_bytes=64)
                live["z", b] = z_bf
            rows = slice(h * P, (h + 1) * P)
            nc.vector.tensor_tensor(
                out=live["z", b][:, s, rows, :],
                in0=live.pop(("acc", b, s, h))[:].rearrange("p j n -> p n j"),
                in1=bias[:, s, rows, :],
                op=ALU.add,
            )

        def relu(b, s, h0, h1, on_vector):
            if ("e", b) not in live:
                e_bf = work.tile([P, 2, T, 4], BF16, name="e_bf", tag="e_bf", align_bytes=64)
                live["e", b] = e_bf
            src = live["z", b][:, s, h0 * P : h1 * P, :].rearrange("p n j -> p (n j)")
            dst = live["e", b][:, s, h0 * P : h1 * P, :].rearrange("p n j -> p (n j)")
            if on_vector:
                nc.vector.tensor_scalar(out=dst, in0=src, scalar1=0.0, scalar2=None, op0=ALU.max)
            else:
                nc.scalar.activation(out=dst, in_=src, func=ACT.Relu)

        def scores(b):
            codes, scales = live.pop(("eq", b))
            sc = ps_s.tile([P, 2, T], F32, name="sc", tag="sc")
            for i in range(2):
                cols = slice(T + i * P, T + (i + 1) * P)
                nc.tensor.matmul_mx(
                    out=sc[:, i, :],
                    lhsT=codes[:, cols].bitcast(FP8X4),
                    lhsT_scale=scales[:, cols],
                    rhs=codes[:, 0:T].bitcast(FP8X4),
                    rhs_scale=scales[:, 0:T],
                    start=True,
                    stop=True,
                )
            live["sc", b] = sc

        def row_max(b):
            neg_max = work.tile([P, 2], F32, name="neg_max", tag="neg_max")
            nc.vector.tensor_reduce(out=neg_max[:], in_=live["sc", b][:], axis=AX.X, op=ALU.max, negate=True)
            live["nm", b] = neg_max

        def exps(b):
            sc = live.pop(("sc", b))
            neg_max = live.pop(("nm", b))
            ex = work.tile([P, 2, T], F32, name="ex", tag="ex")
            sums = work.tile([P, 2], F32, name="sums", tag="sums")
            for i in range(2):
                nc.scalar.activation(
                    out=ex[:, i, :], in_=sc[:, i, :], func=ACT.Exp, bias=neg_max[:, i : i + 1], accum_out=sums[:, i : i + 1]
                )
            live["ex", b] = ex
            live["sums", b] = sums

        def recip(b):
            inv = work.tile([P, 2], F32, name="inv", tag="inv")
            nc.vector.reciprocal(out=inv[:], in_=live.pop(("sums", b))[:])
            live["inv", b] = inv

        def normalise(b):
            ex = live.pop(("ex", b))
            inv = live.pop(("inv", b))
            probs = work.tile([P, 2, T], F32, name="probs", tag="probs")
            for i in range(2):
                nc.scalar.activation(out=probs[:, i, :], in_=ex[:, i, :], func=ACT.Copy, scale=inv[:, i : i + 1])
            nc.sync.dma_start(out=out[b].rearrange("(r i) j -> r i j", i=2), in_=probs[:])

        with tc.manual_schedule():
            nc.vector.memset(ws_in[:].rearrange("p s n -> p (s n)").bitcast(I32), 0)
            make_identity(nc, ident[:])
            nc.gpsimd.tensor_copy(out=ident_bf[:], in_=ident[:])
            load(0)
            nc.sync.dma_start(out=scale_cols[:], in_=x2_scale.rearrange("a c (p t) -> p (a c t)", t=4))
            nc.sync.dma_start(out=bias_raw[:, 0], in_=b1.rearrange("(i r) k -> r i k", i=2))
            nc.sync.dma_start(out=bias_raw[:, 1], in_=b2.rearrange("(r i) k -> r i k", i=2))
            nc.sync.dma_start(out=w_in[:, 0, :], in_=W1_words[0])
            nc.sync.dma_start(out=w_in[:, 1, :], in_=W2_words[0])
            for s, w_s in enumerate((W1_scales, W2_scales)):
                for q in range(4):
                    nc.sync.dma_start(
                        out=ws_in[32 * q : 32 * q + 4, s, :].bitcast(I32), in_=w_s[0, 4 * q : 4 * q + 4, :].bitcast(I32)
                    )
            for b in range(1, AHEAD_LOAD):
                load(b)
            for s in range(2):
                empty_words(transpose_rows(bias_raw[:, s], s), bias[:, s])
            for s in range(2):
                nc.vector.tensor_copy(
                    out=w_codes[:, s, :].rearrange("p (j m c) -> p j m c", j=4, c=2),
                    in_=w_in[:, s, :].rearrange("p (m j c) -> p j m c", j=4, c=2),
                )
                nc.vector.tensor_copy(
                    out=w_scales[:, s, :].rearrange("p (j m) -> p j m", j=4),
                    in_=ws_in[:, s, :].rearrange("p (m j) -> p j m", j=4),
                )

            def ok(b):
                return 0 <= b < B

            for i in range(-5, B + 3):
                if ok(i + AHEAD_LOAD) and i >= 0:
                    load(i + AHEAD_LOAD)
                if ok(i + 2):
                    exit_x1(i + 2)
                    exit_scale(i + 2)
                    interleave(i + 2)
                if ok(i + 3):
                    transpose_x(i + 3)
                if ok(i - 2):
                    normalise(i - 2)
                if ok(i + 4):
                    widen(i + 4)
                if ok(i):
                    for s in range(2):
                        for h in range(2):
                            add_bias(i, s, h)
                if ok(i - 1):
                    row_max(i - 1)
                    exps(i - 1)
                if ok(i + 2):
                    exit_hop(i + 2)
                if ok(i):
                    relu(i, 0, 0, 2, True)
                if ok(i + 1):
                    live["xq", i + 1] = new_codes()
                    quantize_part(live.pop(("xb", i + 1)), live["xq", i + 1], 0, 2)
                    for s in range(2):
                        for h in range(2):
                            matmul_e(i + 1, s, h)
                if ok(i):
                    relu(i, 1, 0, 2, True)
                    live["eq", i] = new_codes()
                    quantize_part(live["e", i], live["eq", i], 0, 1)
                if ok(i - 1):
                    recip(i - 1)
                if ok(i):
                    quantize_part(live.pop(("e", i)), live["eq", i], 1, 2)
                    scores(i)
